import numpy as np
import ml_dtypes


def mxq(x, axis, fmt="e4m3"):
    dtype, down = {"e4m3": (ml_dtypes.float8_e4m3fn, 7), "e5m2": (ml_dtypes.float8_e5m2, 14)}[fmt]
    v = np.moveaxis(np.asarray(x, np.float32).astype(ml_dtypes.bfloat16).astype(np.float64), axis, -1)
    blocks = v.reshape(v.shape[:-1] + (-1, 32))
    amax = np.abs(blocks).max(-1, keepdims=True)
    byte = np.maximum(np.where(amax > 0, np.frexp(amax)[1] - 1 + 127, 0) - down, 1)
    scale = np.exp2(byte - 127.0)
    codes = (blocks / scale).astype(np.float32).astype(dtype).astype(np.float64)
    return np.moveaxis((codes * scale).reshape(v.shape), -1, axis)


WIDE = False


def mx_kscale(k):
    if not WIDE:
        return np.ones(k)
    levels = np.array([10, -10, 5, -5, 0])
    a = np.random.permutation(np.resize(levels, k // 512 * 4)).reshape(k // 512, 4)
    idx = np.arange(k)
    return np.exp2(a[idx // 512, idx % 128 // 32])


BF16 = ml_dtypes.bfloat16


def bf(x):
    return np.asarray(x, np.float32).astype(BF16)


def f64(x):
    return np.asarray(x).astype(np.float64)


E2M1 = np.array([0.0, 0.5, 1.0, 1.5, 2.0, 3.0, 4.0, 6.0, -0.0, -0.5, -1.0, -1.5, -2.0, -3.0, -4.0, -6.0])


def pack_weight(w, fmt):
    k, n = w.shape
    w = f64(bf(w)).reshape(k // 32, 32, n)
    amax = np.abs(w).max(1)
    if fmt == "e4m3":
        byte = np.frexp(amax)[1] - 1 + 127 - 7
    else:
        mant, ex = np.frexp(amax / 6.0)
        byte = np.where(mant > 0.5, ex, ex - 1) + 127
    byte = np.clip(np.where(amax > 0, byte, 1), 1, 254)
    scaled = (w * np.exp2(127.0 - byte)[:, None, :]).reshape(k, n).astype(np.float32)
    by_word = np.ascontiguousarray(scaled.reshape(k // 512, 128, 4, n).transpose(0, 1, 3, 2))
    if fmt == "e4m3":
        words = by_word.astype(ml_dtypes.float8_e4m3fn).view(np.uint8)
    else:
        c = by_word.astype(ml_dtypes.float4_e2m1fn).view(np.uint8) & 0xF
        words = c[..., 0::2] | (c[..., 1::2] << 4)
    return np.ascontiguousarray(words), np.ascontiguousarray(byte.astype(np.uint8).reshape(k // 512, 16, n))


def unpack_weight(words, scales, fmt):
    g, p, n, _ = words.shape
    if fmt == "e4m3":
        vals = np.ascontiguousarray(words).view(ml_dtypes.float8_e4m3fn).astype(np.float64)
    else:
        nib = np.empty((g, p, n, 4), np.uint8)
        nib[..., 0::2] = words & 0xF
        nib[..., 1::2] = words >> 4
        vals = E2M1[nib]
    vals = vals * np.repeat(np.exp2(scales.astype(np.float64) - 127.0), 8, axis=1)[..., None]
    return vals.transpose(0, 1, 3, 2).reshape(g * 512, n)


B, C, H, W = 4, 512, 32, 32
GAMMA_INIT = 0.1


def setup_inputs():
    t = np.exp2(np.round(np.log2(mx_kscale(C)) / 2))
    gain = np.exp(0.5 * np.random.standard_normal((B, 1, H, W)))
    x = np.random.standard_normal((B, C, H, W)) * gain * t[None, :, None, None]
    gamma = (GAMMA_INIT * np.eye(C) + np.abs(np.random.standard_normal((C, C))) / C) / (t * t)[None, :]
    beta = 0.5 + np.random.random(C)
    gamma_words, gamma_scales = pack_weight(np.ascontiguousarray(gamma.T), "e4m3")
    return {"x": bf(x), "gamma_words": gamma_words, "gamma_scales": gamma_scales, "beta": bf(beta)}


def reference(x, gamma_words, gamma_scales, beta):
    xf = f64(x)
    sq = (xf * xf).reshape(B, C, H * W)
    norm = (unpack_weight(gamma_words, gamma_scales, "e4m3").T @ mxq(sq, 1, "e4m3")) + f64(beta)[None, :, None]
    return xf / np.sqrt(norm.reshape(B, C, H, W))

@@ -1,0 +1,114 @@
+from contextlib import ExitStack
+
+import concourse.mybir as mybir
+
+FP8X4 = mybir.dt.float8_e4m3fn_x4
+BF16 = mybir.dt.bfloat16
+F32 = mybir.dt.float32
+I32 = mybir.dt.int32
+U32 = mybir.dt.uint32
+U8 = mybir.dt.uint8
+ACT = mybir.ActivationFunctionType
+ALU = mybir.AluOpType
+
+P = 128
+PACK = 4
+BATCH, CHANNELS, PIXELS = 4, 512, 32 * 32
+N_TILE = 512
+HALVES = PIXELS // N_TILE
+M_TILES = CHANNELS // P
+QUADRANT = 32
+VECTOR_PIXELS = 256
+
+FLOPS = 2 * BATCH * PIXELS * CHANNELS * CHANNELS
+
+
+def tile_gdn_kernel(tc, x, gamma_words, gamma_scales, beta, out):
+    nc = tc.nc
+    with ExitStack() as ctx:
+        const = ctx.enter_context(tc.tile_pool(name="const", bufs=1))
+        images = ctx.enter_context(tc.tile_pool(name="images", bufs=BATCH))
+        stage = ctx.enter_context(tc.tile_pool(name="stage", bufs=3))
+        roots = ctx.enter_context(tc.tile_pool(name="roots", bufs=6))
+        psum = ctx.enter_context(tc.psum_pool(name="psum", bufs=8))
+
+        one = const.tile([P, 1], F32)
+        nc.vector.memset(one[:], 1.0)
+        warm = const.tile([P, 1], F32)
+        nc.scalar.activation(out=warm[:], in_=one[:], func=ACT.Abs_reciprocal_sqrt)
+
+        g_scales = const.tile([P, CHANNELS], U8, align_bytes=64)
+        nc.vector.memset(g_scales[:].bitcast(I32), 0)
+        for quad in range(P // QUADRANT):
+            nc.sync.dma_start(
+                out=g_scales[QUADRANT * quad : QUADRANT * quad + PACK, :].bitcast(I32),
+                in_=gamma_scales[0, PACK * quad : PACK * (quad + 1), :].bitcast(I32),
+            )
+
+        g_codes = const.tile([P, CHANNELS], U32, align_bytes=64)
+        nc.sync.dma_start(
+            out=g_codes[:].bitcast(I32),
+            in_=gamma_words[0].rearrange("p n t -> p (n t)").bitcast(I32),
+        )
+
+        x_contract = []
+        x_output = []
+        for b in range(BATCH):
+            xc = images.tile([P, PACK, PIXELS], BF16)
+            nc.sync.dma_start(out=xc[:], in_=x[b].rearrange("(p j) h w -> p j (h w)", j=PACK))
+            x_contract.append(xc)
+            xo = images.tile([P, M_TILES, PIXELS], BF16)
+            nc.sync.dma_start(out=xo[:], in_=x[b].rearrange("(m q) h w -> q m (h w)", q=P))
+            x_output.append(xo)
+
+        beta_bf16 = const.tile([P, M_TILES], BF16)
+        with nc.allow_non_contiguous_dma(reason="512 two-byte elements, once"):
+            nc.scalar.dma_start(out=beta_bf16[:], in_=beta.rearrange("(m q) -> q m", q=P))
+        beta_f32 = const.tile([P, M_TILES], F32)
+        nc.vector.tensor_copy(out=beta_f32[:], in_=beta_bf16[:])
+
+        for b in range(BATCH):
+            result = images.tile([P, M_TILES, PIXELS], F32)
+            for h in range(HALVES):
+                pix = slice(N_TILE * h, N_TILE * (h + 1))
+                by_pixel = x_contract[b][:, :, pix].rearrange("p j w -> p w j")
+                squares = stage.tile([P, N_TILE, PACK], BF16, align_bytes=64)
+                nc.vector.tensor_tensor(
+                    out=squares[:, :VECTOR_PIXELS, :],
+                    in0=by_pixel[:, :VECTOR_PIXELS, :],
+                    in1=by_pixel[:, :VECTOR_PIXELS, :],
+                    op=ALU.mult,
+                )
+                nc.scalar.activation(
+                    out=squares[:, VECTOR_PIXELS:, :], in_=by_pixel[:, VECTOR_PIXELS:, :], func=ACT.Square
+                )
+                s_codes = stage.tile([P, N_TILE], U32, align_bytes=64)
+                s_scales = stage.tile([P, N_TILE], U8, align_bytes=64)
+                nc.vector.quantize_mx(
+                    out=s_codes[:].bitcast(FP8X4),
+                    scales=s_scales[:],
+                    in_=squares[:].rearrange("p w j -> p (w j)"),
+                )
+                for m in range(M_TILES):
+                    group = slice(P * m, P * (m + 1))
+                    norm = psum.tile([P, N_TILE], F32)
+                    nc.tensor.matmul_mx(
+                        out=norm[:],
+                        lhsT=g_codes[:, group].bitcast(FP8X4),
+                        lhsT_scale=g_scales[:, group],
+                        rhs=s_codes[:].bitcast(FP8X4),
+                        rhs_scale=s_scales[:],
+                        start=True,
+                        stop=True,
+                    )
+                    inv_root = roots.tile([P, N_TILE], F32)
+                    nc.scalar.activation(
+                        out=inv_root[:], in_=norm[:], func=ACT.Abs_reciprocal_sqrt, bias=beta_f32[:, m : m + 1]
+                    )
+                    nc.vector.tensor_tensor(
+                        out=result[:, m, pix], in0=x_output[b][:, m, pix], in1=inv_root[:], op=ALU.mult
+                    )
+            for m in range(M_TILES):
+                nc.sync.dma_start(
+                    out=out[b, P * m : P * (m + 1)].rearrange("q h w -> q (h w)"), in_=result[:, m, :]
+                )

@@ -18,7 +18,8 @@ N_TILE = 512
 HALVES = PIXELS // N_TILE
 M_TILES = CHANNELS // P
 QUADRANT = 32
-VECTOR_PIXELS = 256
+RUN = 4
+VECTOR_PIXELS = 512
 
 FLOPS = 2 * BATCH * PIXELS * CHANNELS * CHANNELS
 
@@ -26,17 +27,84 @@ FLOPS = 2 * BATCH * PIXELS * CHANNELS * CHANNELS
 def tile_gdn_kernel(tc, x, gamma_words, gamma_scales, beta, out):
     nc = tc.nc
     with ExitStack() as ctx:
+        ctx.enter_context(tc.manual_schedule())
         const = ctx.enter_context(tc.tile_pool(name="const", bufs=1))
         images = ctx.enter_context(tc.tile_pool(name="images", bufs=BATCH))
-        stage = ctx.enter_context(tc.tile_pool(name="stage", bufs=3))
-        roots = ctx.enter_context(tc.tile_pool(name="roots", bufs=6))
+        stage = ctx.enter_context(tc.tile_pool(name="stage", bufs=2))
+        roots = ctx.enter_context(tc.tile_pool(name="roots", bufs=4))
+        results = ctx.enter_context(tc.tile_pool(name="results", bufs=BATCH * M_TILES))
         psum = ctx.enter_context(tc.psum_pool(name="psum", bufs=8))
+
+        x_contract = {}
+        x_output = {}
+        codes = {}
+        scales = {}
+
+        def load_for_contraction(b, pieces):
+            xc = images.tile([P, PACK, PIXELS], BF16)
+            source = x[b].rearrange("(p j) h w -> p j (h w)", j=PACK)
+            width = PIXELS // pieces
+            for piece in range(pieces):
+                pix = slice(width * piece, width * (piece + 1))
+                nc.sync.dma_start(out=xc[:, :, pix], in_=source[:, :, pix])
+            x_contract[b] = xc
+
+        def load_for_output(b):
+            xo = images.tile([P, M_TILES, PIXELS], BF16)
+            nc.sync.dma_start(out=xo[:], in_=x[b].rearrange("(m q) h w -> q m (h w)", q=P))
+            x_output[b] = xo
+
+        def quantise_squares(b):
+            squares = stage.tile([P, PIXELS, PACK], BF16, align_bytes=64)
+            source = x_contract[b][:].rearrange("p j (c i) -> p c j i", i=RUN)
+            target = squares[:].rearrange("p (c i) j -> p c j i", i=RUN)
+            cut = VECTOR_PIXELS // RUN
+            nc.vector.tensor_tensor(out=target[:, :cut], in0=source[:, :cut], in1=source[:, :cut], op=ALU.mult)
+            nc.scalar.activation(out=target[:, cut:], in_=source[:, cut:], func=ACT.Square)
+            s_codes = stage.tile([P, PIXELS], U32, align_bytes=64)
+            s_scales = stage.tile([P, PIXELS], U8, align_bytes=64)
+            for h in range(HALVES):
+                pix = slice(N_TILE * h, N_TILE * (h + 1))
+                nc.vector.quantize_mx(
+                    out=s_codes[:, pix].bitcast(FP8X4),
+                    scales=s_scales[:, pix],
+                    in_=squares[:, pix, :].rearrange("p w j -> p (w j)"),
+                )
+            codes[b] = s_codes
+            scales[b] = s_scales
+
+        def normalise_group(b, m):
+            group = slice(P * m, P * (m + 1))
+            inv_root = roots.tile([P, PIXELS], F32)
+            for h in range(HALVES):
+                pix = slice(N_TILE * h, N_TILE * (h + 1))
+                norm = psum.tile([P, N_TILE], F32)
+                nc.tensor.matmul_mx(
+                    out=norm[:],
+                    lhsT=g_codes[:, group].bitcast(FP8X4),
+                    lhsT_scale=g_scales[:, group],
+                    rhs=codes[b][:, pix].bitcast(FP8X4),
+                    rhs_scale=scales[b][:, pix],
+                    start=True,
+                    stop=True,
+                )
+                nc.scalar.activation(
+                    out=inv_root[:, pix], in_=norm[:], func=ACT.Abs_reciprocal_sqrt, bias=beta_bf16[:, m : m + 1]
+                )
+            result = results.tile([P, PIXELS], F32)
+            nc.vector.tensor_tensor(out=result[:], in0=x_output[b][:, m, :], in1=inv_root[:], op=ALU.mult)
+            nc.sync.dma_start(out=out[b, group].rearrange("q h w -> q (h w)"), in_=result[:])
 
         one = const.tile([P, 1], F32)
         nc.vector.memset(one[:], 1.0)
         warm = const.tile([P, 1], F32)
         nc.scalar.activation(out=warm[:], in_=one[:], func=ACT.Abs_reciprocal_sqrt)
 
+        beta_bf16 = const.tile([P, M_TILES], BF16)
+        with nc.allow_non_contiguous_dma(reason="512 two-byte elements, once"):
+            nc.scalar.dma_start(out=beta_bf16[:], in_=beta.rearrange("(m q) -> q m", q=P))
+
+        load_for_contraction(0, pieces=HALVES)
         g_scales = const.tile([P, CHANNELS], U8, align_bytes=64)
         nc.vector.memset(g_scales[:].bitcast(I32), 0)
         for quad in range(P // QUADRANT):
@@ -44,71 +112,18 @@ def tile_gdn_kernel(tc, x, gamma_words, gamma_scales, beta, out):
                 out=g_scales[QUADRANT * quad : QUADRANT * quad + PACK, :].bitcast(I32),
                 in_=gamma_scales[0, PACK * quad : PACK * (quad + 1), :].bitcast(I32),
             )
-
         g_codes = const.tile([P, CHANNELS], U32, align_bytes=64)
         nc.sync.dma_start(
-            out=g_codes[:].bitcast(I32),
-            in_=gamma_words[0].rearrange("p n t -> p (n t)").bitcast(I32),
+            out=g_codes[:].bitcast(I32), in_=gamma_words[0].rearrange("p n t -> p (n t)").bitcast(I32)
         )
-
-        x_contract = []
-        x_output = []
         for b in range(BATCH):
-            xc = images.tile([P, PACK, PIXELS], BF16)
-            nc.sync.dma_start(out=xc[:], in_=x[b].rearrange("(p j) h w -> p j (h w)", j=PACK))
-            x_contract.append(xc)
-            xo = images.tile([P, M_TILES, PIXELS], BF16)
-            nc.sync.dma_start(out=xo[:], in_=x[b].rearrange("(m q) h w -> q m (h w)", q=P))
-            x_output.append(xo)
+            if b + 1 < BATCH:
+                load_for_contraction(b + 1, pieces=1)
+            load_for_output(b)
 
-        beta_bf16 = const.tile([P, M_TILES], BF16)
-        with nc.allow_non_contiguous_dma(reason="512 two-byte elements, once"):
-            nc.scalar.dma_start(out=beta_bf16[:], in_=beta.rearrange("(m q) -> q m", q=P))
-        beta_f32 = const.tile([P, M_TILES], F32)
-        nc.vector.tensor_copy(out=beta_f32[:], in_=beta_bf16[:])
-
+        quantise_squares(0)
         for b in range(BATCH):
-            result = images.tile([P, M_TILES, PIXELS], F32)
-            for h in range(HALVES):
-                pix = slice(N_TILE * h, N_TILE * (h + 1))
-                by_pixel = x_contract[b][:, :, pix].rearrange("p j w -> p w j")
-                squares = stage.tile([P, N_TILE, PACK], BF16, align_bytes=64)
-                nc.vector.tensor_tensor(
-                    out=squares[:, :VECTOR_PIXELS, :],
-                    in0=by_pixel[:, :VECTOR_PIXELS, :],
-                    in1=by_pixel[:, :VECTOR_PIXELS, :],
-                    op=ALU.mult,
-                )
-                nc.scalar.activation(
-                    out=squares[:, VECTOR_PIXELS:, :], in_=by_pixel[:, VECTOR_PIXELS:, :], func=ACT.Square
-                )
-                s_codes = stage.tile([P, N_TILE], U32, align_bytes=64)
-                s_scales = stage.tile([P, N_TILE], U8, align_bytes=64)
-                nc.vector.quantize_mx(
-                    out=s_codes[:].bitcast(FP8X4),
-                    scales=s_scales[:],
-                    in_=squares[:].rearrange("p w j -> p (w j)"),
-                )
-                for m in range(M_TILES):
-                    group = slice(P * m, P * (m + 1))
-                    norm = psum.tile([P, N_TILE], F32)
-                    nc.tensor.matmul_mx(
-                        out=norm[:],
-                        lhsT=g_codes[:, group].bitcast(FP8X4),
-                        lhsT_scale=g_scales[:, group],
-                        rhs=s_codes[:].bitcast(FP8X4),
-                        rhs_scale=s_scales[:],
-                        start=True,
-                        stop=True,
-                    )
-                    inv_root = roots.tile([P, N_TILE], F32)
-                    nc.scalar.activation(
-                        out=inv_root[:], in_=norm[:], func=ACT.Abs_reciprocal_sqrt, bias=beta_f32[:, m : m + 1]
-                    )
-                    nc.vector.tensor_tensor(
-                        out=result[:, m, pix], in0=x_output[b][:, m, pix], in1=inv_root[:], op=ALU.mult
-                    )
+            if b + 1 < BATCH:
+                quantise_squares(b + 1)
             for m in range(M_TILES):
-                nc.sync.dma_start(
-                    out=out[b, P * m : P * (m + 1)].rearrange("q h w -> q (h w)"), in_=result[:, m, :]
-                )
+                normalise_group(b, m)

@@ -19,7 +19,7 @@ HALVES = PIXELS // N_TILE
 M_TILES = CHANNELS // P
 QUADRANT = 32
 RUN = 4
-VECTOR_PIXELS = 512
+VECTOR_PIXELS = 416
 
 FLOPS = 2 * BATCH * PIXELS * CHANNELS * CHANNELS
 
@@ -31,6 +31,7 @@ def tile_gdn_kernel(tc, x, gamma_words, gamma_scales, beta, out):
         const = ctx.enter_context(tc.tile_pool(name="const", bufs=1))
         images = ctx.enter_context(tc.tile_pool(name="images", bufs=BATCH))
         stage = ctx.enter_context(tc.tile_pool(name="stage", bufs=2))
+        operands = ctx.enter_context(tc.tile_pool(name="operands", bufs=BATCH))
         roots = ctx.enter_context(tc.tile_pool(name="roots", bufs=4))
         results = ctx.enter_context(tc.tile_pool(name="results", bufs=BATCH * M_TILES))
         psum = ctx.enter_context(tc.psum_pool(name="psum", bufs=8))
@@ -61,8 +62,8 @@ def tile_gdn_kernel(tc, x, gamma_words, gamma_scales, beta, out):
             cut = VECTOR_PIXELS // RUN
             nc.vector.tensor_tensor(out=target[:, :cut], in0=source[:, :cut], in1=source[:, :cut], op=ALU.mult)
             nc.scalar.activation(out=target[:, cut:], in_=source[:, cut:], func=ACT.Square)
-            s_codes = stage.tile([P, PIXELS], U32, align_bytes=64)
-            s_scales = stage.tile([P, PIXELS], U8, align_bytes=64)
+            s_codes = operands.tile([P, PIXELS], U32, align_bytes=64)
+            s_scales = operands.tile([P, PIXELS], U8, align_bytes=64)
             for h in range(HALVES):
                 pix = slice(N_TILE * h, N_TILE * (h + 1))
                 nc.vector.quantize_mx(
@@ -116,14 +117,13 @@ def tile_gdn_kernel(tc, x, gamma_words, gamma_scales, beta, out):
         nc.sync.dma_start(
             out=g_codes[:].bitcast(I32), in_=gamma_words[0].rearrange("p n t -> p (n t)").bitcast(I32)
         )
+        for b in range(1, BATCH):
+            load_for_contraction(b, pieces=1)
         for b in range(BATCH):
-            if b + 1 < BATCH:
-                load_for_contraction(b + 1, pieces=1)
             load_for_output(b)
 
-        quantise_squares(0)
         for b in range(BATCH):
-            if b + 1 < BATCH:
-                quantise_squares(b + 1)
+            quantise_squares(b)
+        for b in range(BATCH):
             for m in range(M_TILES):
                 normalise_group(b, m)

@@ -1,6 +1,7 @@
 from contextlib import ExitStack
 
 import concourse.mybir as mybir
+from concourse.masks import make_identity
 
 FP8X4 = mybir.dt.float8_e4m3fn_x4
 BF16 = mybir.dt.bfloat16
@@ -19,7 +20,7 @@ HALVES = PIXELS // N_TILE
 M_TILES = CHANNELS // P
 QUADRANT = 32
 RUN = 4
-VECTOR_PIXELS = 416
+VECTOR_PIXELS = 384
 
 FLOPS = 2 * BATCH * PIXELS * CHANNELS * CHANNELS
 
@@ -41,13 +42,9 @@ def tile_gdn_kernel(tc, x, gamma_words, gamma_scales, beta, out):
         codes = {}
         scales = {}
 
-        def load_for_contraction(b, pieces):
+        def load_for_contraction(b):
             xc = images.tile([P, PACK, PIXELS], BF16)
-            source = x[b].rearrange("(p j) h w -> p j (h w)", j=PACK)
-            width = PIXELS // pieces
-            for piece in range(pieces):
-                pix = slice(width * piece, width * (piece + 1))
-                nc.sync.dma_start(out=xc[:, :, pix], in_=source[:, :, pix])
+            nc.sync.dma_start(out=xc[:], in_=x[b].rearrange("(p j) h w -> p j (h w)", j=PACK))
             x_contract[b] = xc
 
         def load_for_output(b):
@@ -64,13 +61,9 @@ def tile_gdn_kernel(tc, x, gamma_words, gamma_scales, beta, out):
             nc.scalar.activation(out=target[:, cut:], in_=source[:, cut:], func=ACT.Square)
             s_codes = operands.tile([P, PIXELS], U32, align_bytes=64)
             s_scales = operands.tile([P, PIXELS], U8, align_bytes=64)
-            for h in range(HALVES):
-                pix = slice(N_TILE * h, N_TILE * (h + 1))
-                nc.vector.quantize_mx(
-                    out=s_codes[:, pix].bitcast(FP8X4),
-                    scales=s_scales[:, pix],
-                    in_=squares[:, pix, :].rearrange("p w j -> p (w j)"),
-                )
+            nc.vector.quantize_mx(
+                out=s_codes[:].bitcast(FP8X4), scales=s_scales[:], in_=squares[:].rearrange("p w j -> p (w j)")
+            )
             codes[b] = s_codes
             scales[b] = s_scales
 
@@ -90,7 +83,7 @@ def tile_gdn_kernel(tc, x, gamma_words, gamma_scales, beta, out):
                     stop=True,
                 )
                 nc.scalar.activation(
-                    out=inv_root[:, pix], in_=norm[:], func=ACT.Abs_reciprocal_sqrt, bias=beta_bf16[:, m : m + 1]
+                    out=inv_root[:, pix], in_=norm[:], func=ACT.Abs_reciprocal_sqrt, bias=beta_columns[:, m : m + 1]
                 )
             result = results.tile([P, PIXELS], F32)
             nc.vector.tensor_tensor(out=result[:], in0=x_output[b][:, m, :], in1=inv_root[:], op=ALU.mult)
@@ -101,11 +94,17 @@ def tile_gdn_kernel(tc, x, gamma_words, gamma_scales, beta, out):
         warm = const.tile([P, 1], F32)
         nc.scalar.activation(out=warm[:], in_=one[:], func=ACT.Abs_reciprocal_sqrt)
 
-        beta_bf16 = const.tile([P, M_TILES], BF16)
-        with nc.allow_non_contiguous_dma(reason="512 two-byte elements, once"):
-            nc.scalar.dma_start(out=beta_bf16[:], in_=beta.rearrange("(m q) -> q m", q=P))
+        identity = const.tile([P, P], BF16)
+        make_identity(nc, identity[:])
+        beta_rows = const.tile([P, P], BF16)
+        nc.vector.memset(beta_rows[:], 0.0)
+        nc.scalar.dma_start(out=beta_rows[:M_TILES, :], in_=beta.rearrange("(m q) -> m q", q=P))
+        beta_turned = psum.tile([P, P], BF16, tag="norm")
+        nc.tensor.transpose(beta_turned[:], beta_rows[:], identity[:])
+        beta_columns = const.tile([P, M_TILES], F32)
+        nc.scalar.copy(out=beta_columns[:], in_=beta_turned[:, :M_TILES])
 
-        load_for_contraction(0, pieces=HALVES)
+        load_for_contraction(0)
         g_scales = const.tile([P, CHANNELS], U8, align_bytes=64)
         nc.vector.memset(g_scales[:].bitcast(I32), 0)
         for quad in range(P // QUADRANT):
@@ -118,7 +117,7 @@ def tile_gdn_kernel(tc, x, gamma_words, gamma_scales, beta, out):
             out=g_codes[:].bitcast(I32), in_=gamma_words[0].rearrange("p n t -> p (n t)").bitcast(I32)
         )
         for b in range(1, BATCH):
-            load_for_contraction(b, pieces=1)
+            load_for_contraction(b)
         for b in range(BATCH):
             load_for_output(b)
 

@@ -1,7 +1,6 @@
 from contextlib import ExitStack
 
 import concourse.mybir as mybir
-from concourse.masks import make_identity
 
 FP8X4 = mybir.dt.float8_e4m3fn_x4
 BF16 = mybir.dt.bfloat16
@@ -16,11 +15,11 @@ P = 128
 PACK = 4
 BATCH, CHANNELS, PIXELS = 4, 512, 32 * 32
 N_TILE = 512
-HALVES = PIXELS // N_TILE
-M_TILES = CHANNELS // P
 QUADRANT = 32
 RUN = 4
-VECTOR_PIXELS = 384
+UNIT_LIST = [(0, 0, N_TILE), (0, N_TILE, N_TILE)] + [(b, 0, PIXELS) for b in range(1, BATCH)]
+UNITS = len(UNIT_LIST)
+VECTOR_SHARE = 0.375
 
 FLOPS = 2 * BATCH * PIXELS * CHANNELS * CHANNELS
 
@@ -30,99 +29,117 @@ def tile_gdn_kernel(tc, x, gamma_words, gamma_scales, beta, out):
     with ExitStack() as ctx:
         ctx.enter_context(tc.manual_schedule())
         const = ctx.enter_context(tc.tile_pool(name="const", bufs=1))
-        images = ctx.enter_context(tc.tile_pool(name="images", bufs=BATCH))
-        stage = ctx.enter_context(tc.tile_pool(name="stage", bufs=2))
-        operands = ctx.enter_context(tc.tile_pool(name="operands", bufs=BATCH))
-        roots = ctx.enter_context(tc.tile_pool(name="roots", bufs=4))
-        results = ctx.enter_context(tc.tile_pool(name="results", bufs=BATCH * M_TILES))
+        images = ctx.enter_context(tc.tile_pool(name="images", bufs=UNITS))
+        stage = ctx.enter_context(tc.tile_pool(name="stage", bufs=3))
+        operands = ctx.enter_context(tc.tile_pool(name="operands", bufs=UNITS))
+        roots = ctx.enter_context(tc.tile_pool(name="roots", bufs=2))
+        results = ctx.enter_context(tc.tile_pool(name="results", bufs=8))
         psum = ctx.enter_context(tc.psum_pool(name="psum", bufs=8))
 
-        x_contract = {}
-        x_output = {}
+        x_unit = {}
+        squares = {}
         codes = {}
         scales = {}
 
-        def load_for_contraction(b):
-            xc = images.tile([P, PACK, PIXELS], BF16)
-            nc.sync.dma_start(out=xc[:], in_=x[b].rearrange("(p j) h w -> p j (h w)", j=PACK))
-            x_contract[b] = xc
+        def hbm_view(tensor, s):
+            b, first, width = UNIT_LIST[s]
+            return tensor[b].rearrange("(p j) h w -> p j (h w)", j=PACK)[:, :, first : first + width]
 
-        def load_for_output(b):
-            xo = images.tile([P, M_TILES, PIXELS], BF16)
-            nc.sync.dma_start(out=xo[:], in_=x[b].rearrange("(m q) h w -> q m (h w)", q=P))
-            x_output[b] = xo
+        def load(s):
+            xu = images.tile([P, PACK, UNIT_LIST[s][2]], BF16)
+            nc.sync.dma_start(out=xu[:], in_=hbm_view(x, s))
+            x_unit[s] = xu
 
-        def quantise_squares(b):
-            squares = stage.tile([P, PIXELS, PACK], BF16, align_bytes=64)
-            source = x_contract[b][:].rearrange("p j (c i) -> p c j i", i=RUN)
-            target = squares[:].rearrange("p (c i) j -> p c j i", i=RUN)
-            cut = VECTOR_PIXELS // RUN
+        def square(s):
+            width = UNIT_LIST[s][2]
+            sq = stage.tile([P, width, PACK], BF16, align_bytes=64)
+            source = x_unit[s][:].rearrange("p j (c i) -> p c j i", i=RUN)
+            target = sq[:].rearrange("p (c i) j -> p c j i", i=RUN)
+            cut = int(width * VECTOR_SHARE) // (2 * RUN) * 2
             nc.vector.tensor_tensor(out=target[:, :cut], in0=source[:, :cut], in1=source[:, :cut], op=ALU.mult)
             nc.scalar.activation(out=target[:, cut:], in_=source[:, cut:], func=ACT.Square)
-            s_codes = operands.tile([P, PIXELS], U32, align_bytes=64)
-            s_scales = operands.tile([P, PIXELS], U8, align_bytes=64)
-            nc.vector.quantize_mx(
-                out=s_codes[:].bitcast(FP8X4), scales=s_scales[:], in_=squares[:].rearrange("p w j -> p (w j)")
-            )
-            codes[b] = s_codes
-            scales[b] = s_scales
+            squares[s] = sq
 
-        def normalise_group(b, m):
-            group = slice(P * m, P * (m + 1))
-            inv_root = roots.tile([P, PIXELS], F32)
-            for h in range(HALVES):
-                pix = slice(N_TILE * h, N_TILE * (h + 1))
-                norm = psum.tile([P, N_TILE], F32)
-                nc.tensor.matmul_mx(
-                    out=norm[:],
-                    lhsT=g_codes[:, group].bitcast(FP8X4),
-                    lhsT_scale=g_scales[:, group],
-                    rhs=codes[b][:, pix].bitcast(FP8X4),
-                    rhs_scale=scales[b][:, pix],
-                    start=True,
-                    stop=True,
-                )
-                nc.scalar.activation(
-                    out=inv_root[:, pix], in_=norm[:], func=ACT.Abs_reciprocal_sqrt, bias=beta_columns[:, m : m + 1]
-                )
-            result = results.tile([P, PIXELS], F32)
-            nc.vector.tensor_tensor(out=result[:], in0=x_output[b][:, m, :], in1=inv_root[:], op=ALU.mult)
-            nc.sync.dma_start(out=out[b, group].rearrange("q h w -> q (h w)"), in_=result[:])
+        def quantise(s):
+            width = UNIT_LIST[s][2]
+            s_codes = operands.tile([P, width], U32, align_bytes=64)
+            s_scales = operands.tile([P, width], U8, align_bytes=64)
+            nc.vector.quantize_mx(
+                out=s_codes[:].bitcast(FP8X4), scales=s_scales[:], in_=squares[s][:].rearrange("p w j -> p (w j)")
+            )
+            codes[s] = s_codes
+            scales[s] = s_scales
+
+        def normalise(s):
+            width = UNIT_LIST[s][2]
+            inv_root = roots.tile([P, PACK, width], F32)
+            for t in range(PACK):
+                group = slice(P * t, P * (t + 1))
+                step = N_TILE if (s == UNITS - 1 and t == PACK - 1) else width
+                for first in range(0, width, N_TILE):
+                    pix = slice(first, first + N_TILE)
+                    norm = psum.tile([P, N_TILE], F32)
+                    nc.tensor.matmul_mx(
+                        out=norm[:],
+                        lhsT=g_codes[:, group].bitcast(FP8X4),
+                        lhsT_scale=g_scales[:, group],
+                        rhs=codes[s][:, pix].bitcast(FP8X4),
+                        rhs_scale=scales[s][:, pix],
+                        start=True,
+                        stop=True,
+                    )
+                    nc.scalar.activation(
+                        out=inv_root[:, t, pix],
+                        in_=norm[:],
+                        func=ACT.Abs_reciprocal_sqrt,
+                        bias=beta_columns[:, t : t + 1],
+                    )
+                    if (first + N_TILE) % step == 0:
+                        done = slice(first + N_TILE - step, first + N_TILE)
+                        result = results.tile([P, step], F32)
+                        nc.vector.tensor_tensor(
+                            out=result[:], in0=x_unit[s][:, t, done], in1=inv_root[:, t, done], op=ALU.mult
+                        )
+                        nc.sync.dma_start(out=hbm_view(out, s)[:, t, done], in_=result[:])
 
         one = const.tile([P, 1], F32)
         nc.vector.memset(one[:], 1.0)
         warm = const.tile([P, 1], F32)
         nc.scalar.activation(out=warm[:], in_=one[:], func=ACT.Abs_reciprocal_sqrt)
 
-        identity = const.tile([P, P], BF16)
-        make_identity(nc, identity[:])
-        beta_rows = const.tile([P, P], BF16)
-        nc.vector.memset(beta_rows[:], 0.0)
-        nc.scalar.dma_start(out=beta_rows[:M_TILES, :], in_=beta.rearrange("(m q) -> m q", q=P))
-        beta_turned = psum.tile([P, P], BF16, tag="norm")
-        nc.tensor.transpose(beta_turned[:], beta_rows[:], identity[:])
-        beta_columns = const.tile([P, M_TILES], F32)
-        nc.scalar.copy(out=beta_columns[:], in_=beta_turned[:, :M_TILES])
+        beta_columns = const.tile([P, PACK], BF16)
+        nc.scalar.dma_start(out=beta_columns[:], in_=beta.rearrange("(p t) -> p t", t=PACK))
 
-        load_for_contraction(0)
-        g_scales = const.tile([P, CHANNELS], U8, align_bytes=64)
-        nc.vector.memset(g_scales[:].bitcast(I32), 0)
+        for s in range(UNITS):
+            load(s)
+        raw_scales = const.tile([P, CHANNELS], U8, align_bytes=64)
+        nc.vector.memset(raw_scales[:].bitcast(I32), 0)
         for quad in range(P // QUADRANT):
             nc.sync.dma_start(
-                out=g_scales[QUADRANT * quad : QUADRANT * quad + PACK, :].bitcast(I32),
+                out=raw_scales[QUADRANT * quad : QUADRANT * quad + PACK, :].bitcast(I32),
                 in_=gamma_scales[0, PACK * quad : PACK * (quad + 1), :].bitcast(I32),
             )
-        g_codes = const.tile([P, CHANNELS], U32, align_bytes=64)
+        raw_codes = const.tile([P, CHANNELS], U32, align_bytes=64)
         nc.sync.dma_start(
-            out=g_codes[:].bitcast(I32), in_=gamma_words[0].rearrange("p n t -> p (n t)").bitcast(I32)
+            out=raw_codes[:].bitcast(I32), in_=gamma_words[0].rearrange("p n t -> p (n t)").bitcast(I32)
         )
-        for b in range(1, BATCH):
-            load_for_contraction(b)
-        for b in range(BATCH):
-            load_for_output(b)
 
-        for b in range(BATCH):
-            quantise_squares(b)
-        for b in range(BATCH):
-            for m in range(M_TILES):
-                normalise_group(b, m)
+        square(0)
+        for s in range(1, UNITS):
+            square(s)
+            if s < UNITS - 1:
+                quantise(s - 1)
+        g_codes = const.tile([P, CHANNELS], U32, align_bytes=64)
+        nc.vector.tensor_copy(
+            out=g_codes[:].bitcast(I32).rearrange("p (t m) -> p t m", t=PACK),
+            in_=raw_codes[:].bitcast(I32).rearrange("p (m t) -> p t m", t=PACK),
+        )
+        g_scales = const.tile([P, CHANNELS], U8, align_bytes=64)
+        nc.vector.tensor_copy(
+            out=g_scales[:].rearrange("p (t m) -> p m t", t=PACK),
+            in_=raw_scales[:].rearrange("p (m t) -> p m t", t=PACK),
+        )
+        quantise(UNITS - 2)
+        quantise(UNITS - 1)
+        for s in range(UNITS):
+            normalise(s)

@@ -19,7 +19,7 @@ QUADRANT = 32
 RUN = 4
 UNIT_LIST = [(0, 0, N_TILE), (0, N_TILE, N_TILE)] + [(b, 0, PIXELS) for b in range(1, BATCH)]
 UNITS = len(UNIT_LIST)
-VECTOR_SHARE = 0.375
+VECTOR_SHARE = 0.345
 
 FLOPS = 2 * BATCH * PIXELS * CHANNELS * CHANNELS
 

@@ -16,7 +16,7 @@ PACK = 4
 BATCH, CHANNELS, PIXELS = 4, 512, 32 * 32
 N_TILE = 512
 QUADRANT = 32
-RUN = 4
+RUN = 8
 UNIT_LIST = [(0, 0, N_TILE), (0, N_TILE, N_TILE)] + [(b, 0, PIXELS) for b in range(1, BATCH)]
 UNITS = len(UNIT_LIST)
 VECTOR_SHARE = 0.345

@@ -17,7 +17,7 @@ BATCH, CHANNELS, PIXELS = 4, 512, 32 * 32
 N_TILE = 512
 QUADRANT = 32
 RUN = 8
-UNIT_LIST = [(0, 0, N_TILE), (0, N_TILE, N_TILE)] + [(b, 0, PIXELS) for b in range(1, BATCH)]
+UNIT_LIST = [(b, h, N_TILE) for b in (0, 1) for h in (0, N_TILE)] + [(b, 0, PIXELS) for b in (2, 3)]
 UNITS = len(UNIT_LIST)
 VECTOR_SHARE = 0.345
 
@@ -29,31 +29,33 @@ def tile_gdn_kernel(tc, x, gamma_words, gamma_scales, beta, out):
     with ExitStack() as ctx:
         ctx.enter_context(tc.manual_schedule())
         const = ctx.enter_context(tc.tile_pool(name="const", bufs=1))
-        images = ctx.enter_context(tc.tile_pool(name="images", bufs=UNITS))
+        images = ctx.enter_context(tc.tile_pool(name="images", bufs=BATCH))
         stage = ctx.enter_context(tc.tile_pool(name="stage", bufs=3))
-        operands = ctx.enter_context(tc.tile_pool(name="operands", bufs=UNITS))
+        operands = ctx.enter_context(tc.tile_pool(name="operands", bufs=BATCH))
         roots = ctx.enter_context(tc.tile_pool(name="roots", bufs=2))
         results = ctx.enter_context(tc.tile_pool(name="results", bufs=8))
         psum = ctx.enter_context(tc.psum_pool(name="psum", bufs=8))
 
-        x_unit = {}
+        x_image = {}
         squares = {}
         codes = {}
         scales = {}
 
-        def hbm_view(tensor, s):
-            b, first, width = UNIT_LIST[s]
-            return tensor[b].rearrange("(p j) h w -> p j (h w)", j=PACK)[:, :, first : first + width]
+        def hbm_view(tensor, b):
+            return tensor[b].rearrange("(p j) h w -> p j (h w)", j=PACK)
 
         def load(s):
-            xu = images.tile([P, PACK, UNIT_LIST[s][2]], BF16)
-            nc.sync.dma_start(out=xu[:], in_=hbm_view(x, s))
-            x_unit[s] = xu
+            b, first, width = UNIT_LIST[s]
+            if first == 0:
+                xi = images.tile([P, PACK, PIXELS], BF16)
+                x_image[b] = xi
+            pix = slice(first, first + width)
+            nc.sync.dma_start(out=x_image[b][:, :, pix], in_=hbm_view(x, b)[:, :, pix])
 
         def square(s):
-            width = UNIT_LIST[s][2]
+            b, first, width = UNIT_LIST[s]
             sq = stage.tile([P, width, PACK], BF16, align_bytes=64)
-            source = x_unit[s][:].rearrange("p j (c i) -> p c j i", i=RUN)
+            source = x_image[b][:, :, first : first + width].rearrange("p j (c i) -> p c j i", i=RUN)
             target = sq[:].rearrange("p (c i) j -> p c j i", i=RUN)
             cut = int(width * VECTOR_SHARE) // (2 * RUN) * 2
             nc.vector.tensor_tensor(out=target[:, :cut], in0=source[:, :cut], in1=source[:, :cut], op=ALU.mult)
@@ -61,30 +63,33 @@ def tile_gdn_kernel(tc, x, gamma_words, gamma_scales, beta, out):
             squares[s] = sq
 
         def quantise(s):
-            width = UNIT_LIST[s][2]
-            s_codes = operands.tile([P, width], U32, align_bytes=64)
-            s_scales = operands.tile([P, width], U8, align_bytes=64)
+            b, first, width = UNIT_LIST[s]
+            if first == 0:
+                s_codes = operands.tile([P, PIXELS], U32, align_bytes=64)
+                s_scales = operands.tile([P, PIXELS], U8, align_bytes=64)
+                codes[b] = s_codes
+                scales[b] = s_scales
+            pix = slice(first, first + width)
             nc.vector.quantize_mx(
-                out=s_codes[:].bitcast(FP8X4), scales=s_scales[:], in_=squares[s][:].rearrange("p w j -> p (w j)")
+                out=codes[b][:, pix].bitcast(FP8X4),
+                scales=scales[b][:, pix],
+                in_=squares[s][:].rearrange("p w j -> p (w j)"),
             )
-            codes[s] = s_codes
-            scales[s] = s_scales
 
-        def normalise(s):
-            width = UNIT_LIST[s][2]
-            inv_root = roots.tile([P, PACK, width], F32)
+        def normalise(b):
+            inv_root = roots.tile([P, PACK, PIXELS], F32)
             for t in range(PACK):
                 group = slice(P * t, P * (t + 1))
-                step = N_TILE if (s == UNITS - 1 and t == PACK - 1) else width
-                for first in range(0, width, N_TILE):
+                step = N_TILE if (b == BATCH - 1 and t == PACK - 1) else PIXELS
+                for first in range(0, PIXELS, N_TILE):
                     pix = slice(first, first + N_TILE)
                     norm = psum.tile([P, N_TILE], F32)
                     nc.tensor.matmul_mx(
                         out=norm[:],
                         lhsT=g_codes[:, group].bitcast(FP8X4),
                         lhsT_scale=g_scales[:, group],
-                        rhs=codes[s][:, pix].bitcast(FP8X4),
-                        rhs_scale=scales[s][:, pix],
+                        rhs=codes[b][:, pix].bitcast(FP8X4),
+                        rhs_scale=scales[b][:, pix],
                         start=True,
                         stop=True,
                     )
@@ -98,9 +103,9 @@ def tile_gdn_kernel(tc, x, gamma_words, gamma_scales, beta, out):
                         done = slice(first + N_TILE - step, first + N_TILE)
                         result = results.tile([P, step], F32)
                         nc.vector.tensor_tensor(
-                            out=result[:], in0=x_unit[s][:, t, done], in1=inv_root[:, t, done], op=ALU.mult
+                            out=result[:], in0=x_image[b][:, t, done], in1=inv_root[:, t, done], op=ALU.mult
                         )
-                        nc.sync.dma_start(out=hbm_view(out, s)[:, t, done], in_=result[:])
+                        nc.sync.dma_start(out=hbm_view(out, b)[:, t, done], in_=result[:])
 
         one = const.tile([P, 1], F32)
         nc.vector.memset(one[:], 1.0)
@@ -141,5 +146,5 @@ def tile_gdn_kernel(tc, x, gamma_words, gamma_scales, beta, out):
         )
         quantise(UNITS - 2)
         quantise(UNITS - 1)
-        for s in range(UNITS):
-            normalise(s)
+        for b in range(BATCH):
+            normalise(b)

from contextlib import ExitStack

import concourse.mybir as mybir

FP8X4 = mybir.dt.float8_e4m3fn_x4
BF16 = mybir.dt.bfloat16
F32 = mybir.dt.float32
I32 = mybir.dt.int32
U32 = mybir.dt.uint32
U8 = mybir.dt.uint8
ACT = mybir.ActivationFunctionType
ALU = mybir.AluOpType

P = 128
PACK = 4
BATCH, CHANNELS, PIXELS = 4, 512, 32 * 32
N_TILE = 512
QUADRANT = 32
RUN = 8
UNIT_LIST = [(b, h, N_TILE) for b in (0, 1) for h in (0, N_TILE)] + [(b, 0, PIXELS) for b in (2, 3)]
UNITS = len(UNIT_LIST)
VECTOR_SHARE = 0.345

FLOPS = 2 * BATCH * PIXELS * CHANNELS * CHANNELS


def tile_gdn_kernel(tc, x, gamma_words, gamma_scales, beta, out):
    nc = tc.nc
    with ExitStack() as ctx:
        ctx.enter_context(tc.manual_schedule())
        const = ctx.enter_context(tc.tile_pool(name="const", bufs=1))
        images = ctx.enter_context(tc.tile_pool(name="images", bufs=BATCH))
        stage = ctx.enter_context(tc.tile_pool(name="stage", bufs=3))
        operands = ctx.enter_context(tc.tile_pool(name="operands", bufs=BATCH))
        roots = ctx.enter_context(tc.tile_pool(name="roots", bufs=2))
        results = ctx.enter_context(tc.tile_pool(name="results", bufs=8))
        psum = ctx.enter_context(tc.psum_pool(name="psum", bufs=8))

        x_image = {}
        squares = {}
        codes = {}
        scales = {}

        def hbm_view(tensor, b):
            return tensor[b].rearrange("(p j) h w -> p j (h w)", j=PACK)

        def load(s):
            b, first, width = UNIT_LIST[s]
            if first == 0:
                xi = images.tile([P, PACK, PIXELS], BF16)
                x_image[b] = xi
            pix = slice(first, first + width)
            nc.sync.dma_start(out=x_image[b][:, :, pix], in_=hbm_view(x, b)[:, :, pix])

        def square(s):
            b, first, width = UNIT_LIST[s]
            sq = stage.tile([P, width, PACK], BF16, align_bytes=64)
            source = x_image[b][:, :, first : first + width].rearrange("p j (c i) -> p c j i", i=RUN)
            target = sq[:].rearrange("p (c i) j -> p c j i", i=RUN)
            cut = int(width * VECTOR_SHARE) // (2 * RUN) * 2
            nc.vector.tensor_tensor(out=target[:, :cut], in0=source[:, :cut], in1=source[:, :cut], op=ALU.mult)
            nc.scalar.activation(out=target[:, cut:], in_=source[:, cut:], func=ACT.Square)
            squares[s] = sq

        def quantise(s):
            b, first, width = UNIT_LIST[s]
            if first == 0:
                s_codes = operands.tile([P, PIXELS], U32, align_bytes=64)
                s_scales = operands.tile([P, PIXELS], U8, align_bytes=64)
                codes[b] = s_codes
                scales[b] = s_scales
            pix = slice(first, first + width)
            nc.vector.quantize_mx(
                out=codes[b][:, pix].bitcast(FP8X4),
                scales=scales[b][:, pix],
                in_=squares[s][:].rearrange("p w j -> p (w j)"),
            )

        def normalise(b):
            inv_root = roots.tile([P, PACK, PIXELS], F32)
            for t in range(PACK):
                group = slice(P * t, P * (t + 1))
                step = N_TILE if (b == BATCH - 1 and t == PACK - 1) else PIXELS
                for first in range(0, PIXELS, N_TILE):
                    pix = slice(first, first + N_TILE)
                    norm = psum.tile([P, N_TILE], F32)
                    nc.tensor.matmul_mx(
                        out=norm[:],
                        lhsT=g_codes[:, group].bitcast(FP8X4),
                        lhsT_scale=g_scales[:, group],
                        rhs=codes[b][:, pix].bitcast(FP8X4),
                        rhs_scale=scales[b][:, pix],
                        start=True,
                        stop=True,
                    )
                    nc.scalar.activation(
                        out=inv_root[:, t, pix],
                        in_=norm[:],
                        func=ACT.Abs_reciprocal_sqrt,
                        bias=beta_columns[:, t : t + 1],
                    )
                    if (first + N_TILE) % step == 0:
                        done = slice(first + N_TILE - step, first + N_TILE)
                        result = results.tile([P, step], F32)
                        nc.vector.tensor_tensor(
                            out=result[:], in0=x_image[b][:, t, done], in1=inv_root[:, t, done], op=ALU.mult
                        )
                        nc.sync.dma_start(out=hbm_view(out, b)[:, t, done], in_=result[:])

        one = const.tile([P, 1], F32)
        nc.vector.memset(one[:], 1.0)
        warm = const.tile([P, 1], F32)
        nc.scalar.activation(out=warm[:], in_=one[:], func=ACT.Abs_reciprocal_sqrt)

        beta_columns = const.tile([P, PACK], BF16)
        nc.scalar.dma_start(out=beta_columns[:], in_=beta.rearrange("(p t) -> p t", t=PACK))

        for s in range(UNITS):
            load(s)
        raw_scales = const.tile([P, CHANNELS], U8, align_bytes=64)
        nc.vector.memset(raw_scales[:].bitcast(I32), 0)
        for quad in range(P // QUADRANT):
            nc.sync.dma_start(
                out=raw_scales[QUADRANT * quad : QUADRANT * quad + PACK, :].bitcast(I32),
                in_=gamma_scales[0, PACK * quad : PACK * (quad + 1), :].bitcast(I32),
            )
        raw_codes = const.tile([P, CHANNELS], U32, align_bytes=64)
        nc.sync.dma_start(
            out=raw_codes[:].bitcast(I32), in_=gamma_words[0].rearrange("p n t -> p (n t)").bitcast(I32)
        )

        square(0)
        for s in range(1, UNITS):
            square(s)
            if s < UNITS - 1:
                quantise(s - 1)
        g_codes = const.tile([P, CHANNELS], U32, align_bytes=64)
        nc.vector.tensor_copy(
            out=g_codes[:].bitcast(I32).rearrange("p (t m) -> p t m", t=PACK),
            in_=raw_codes[:].bitcast(I32).rearrange("p (m t) -> p t m", t=PACK),
        )
        g_scales = const.tile([P, CHANNELS], U8, align_bytes=64)
        nc.vector.tensor_copy(
            out=g_scales[:].rearrange("p (t m) -> p m t", t=PACK),
            in_=raw_scales[:].rearrange("p (m t) -> p m t", t=PACK),
        )
        quantise(UNITS - 2)
        quantise(UNITS - 1)
        for b in range(BATCH):
            normalise(b)
